import numpy as np
import ml_dtypes


def mxq(x, axis, fmt="e4m3"):
    dtype, down = {"e4m3": (ml_dtypes.float8_e4m3fn, 7), "e5m2": (ml_dtypes.float8_e5m2, 14)}[fmt]
    v = np.moveaxis(np.asarray(x, np.float32).astype(ml_dtypes.bfloat16).astype(np.float64), axis, -1)
    blocks = v.reshape(v.shape[:-1] + (-1, 32))
    amax = np.abs(blocks).max(-1, keepdims=True)
    byte = np.maximum(np.where(amax > 0, np.frexp(amax)[1] - 1 + 127, 0) - down, 1)
    scale = np.exp2(byte - 127.0)
    codes = (blocks / scale).astype(np.float32).astype(dtype).astype(np.float64)
    return np.moveaxis((codes * scale).reshape(v.shape), -1, axis)


WIDE = False


def mx_kscale(k):
    if not WIDE:
        return np.ones(k)
    levels = np.array([10, -10, 5, -5, 0])
    a = np.random.permutation(np.resize(levels, k // 512 * 4)).reshape(k // 512, 4)
    idx = np.arange(k)
    return np.exp2(a[idx // 512, idx % 128 // 32])


BF16 = ml_dtypes.bfloat16


def bf(x):
    return np.asarray(x, np.float32).astype(BF16)


def f64(x):
    return np.asarray(x).astype(np.float64)


B, S, D, DR = 8, 512, 1024, 512
G = 1.4 * (D / DR) ** 0.25 / np.sqrt(D)


def setup_inputs():
    s = mx_kscale(D)
    t = mx_kscale(DR)
    mask = (np.random.random((S, S)) < 0.5) & ~np.eye(S, dtype=bool)
    return {"q_lin": bf(np.random.standard_normal((B, S, D)) * s),
            "k_lin": bf(np.random.standard_normal((B, S, D)) * s),
            "rotation_params": bf(np.random.standard_normal((DR, D)) * G * t[:, None] / s),
            "entangle_params": bf(np.random.standard_normal((DR, D)) * G / t[:, None] / s),
            "mask": mask}


def reference(q_lin, k_lin, rotation_params, entangle_params, mask):
    q = mxq(f64(q_lin), 2, "e4m3") @ mxq(f64(rotation_params), 1, "e4m3").T
    k = mxq(f64(k_lin), 2, "e4m3") @ mxq(f64(entangle_params), 1, "e4m3").T
    scores = (mxq(q, 2, "e4m3") @ mxq(k, 2, "e4m3").transpose(0, 2, 1)) / np.sqrt(D)
    scores = np.where(f64(mask) > 0.5, -np.inf, scores)
    e = np.exp(scores - scores.max(-1, keepdims=True))
    return e / e.sum(-1, keepdims=True)

@@ -1,0 +1,278 @@
+from contextlib import ExitStack
+
+import concourse.mybir as mybir
+from concourse.masks import make_identity
+
+F32 = mybir.dt.float32
+BF16 = mybir.dt.bfloat16
+I32 = mybir.dt.int32
+U32 = mybir.dt.uint32
+U8 = mybir.dt.uint8
+FP8X4 = mybir.dt.float8_e4m3fn_x4
+ALU = mybir.AluOpType
+ACT = mybir.ActivationFunctionType
+
+P = 128
+PACK = 4
+K_PASS = P * PACK
+BANK = 512
+PSUM_BANKS = 8
+
+BATCH = 8
+TOKENS = 512
+WIDTH = 1024
+FEATURES = 512
+CHUNKS = TOKENS // P
+PASSES = WIDTH // K_PASS
+ROW_WORDS = WIDTH // 2
+PASS_WORDS = K_PASS // 2
+UNITS = 2 * BATCH
+PAIR = 2
+PAIRS = BATCH * CHUNKS // PAIR
+PREFETCH = 4
+
+SCORE_SCALE = 1.0 / 32.0
+CAP = 1.0e38
+
+FLOPS = 2 * (2 * BATCH * TOKENS * WIDTH * FEATURES) + 2 * BATCH * TOKENS * TOKENS * FEATURES
+
+
+def tile_selfattention_pa_t_kernel(
+    tc, q_lin, k_lin, rotation_params, entangle_params, mask, out
+):
+    nc = tc.nc
+    with ExitStack() as ctx:
+        const = ctx.enter_context(tc.tile_pool(name="const", bufs=1))
+        rows_pool = ctx.enter_context(tc.tile_pool(name="rows", bufs=PREFETCH + 2))
+        grouped_pool = ctx.enter_context(tc.tile_pool(name="grouped", bufs=2))
+        unit_mx_pool = ctx.enter_context(tc.tile_pool(name="unit_mx", bufs=3))
+        feat_pool = ctx.enter_context(tc.tile_pool(name="feat", bufs=2))
+        feat_mx_pool = ctx.enter_context(tc.tile_pool(name="feat_mx", bufs=6))
+        prob_pool = ctx.enter_context(tc.tile_pool(name="prob", bufs=4))
+        small = ctx.enter_context(tc.tile_pool(name="small", bufs=4))
+        psum = ctx.enter_context(tc.psum_pool(name="psum", bufs=PSUM_BANKS))
+        ctx.enter_context(tc.manual_schedule())
+
+        def load_rows(chunk_views):
+            rows = rows_pool.tile([P, CHUNKS * WIDTH], BF16, name="rows")
+            for c in range(CHUNKS):
+                nc.sync.dma_start(out=rows[:, c * WIDTH : (c + 1) * WIDTH], in_=chunk_views[c])
+            return rows
+
+        def load_unit(unit):
+            source = q_lin if unit % 2 == 0 else k_lin
+            return load_rows([source[unit // 2, c * P : (c + 1) * P, :] for c in range(CHUNKS)])
+
+        def load_weight(weight):
+            by_chunk = weight.rearrange("(p c) d -> c p d", c=CHUNKS)
+            return load_rows([by_chunk[c] for c in range(CHUNKS)])
+
+        def transpose_rows(rows):
+            words = rows[:].bitcast(F32)
+            grouped = grouped_pool.tile(
+                [P, PASSES * TOKENS * PACK], BF16, name="grouped", align_bytes=64
+            )
+            grouped_words = grouped[:].bitcast(F32)
+            for g in range(PASSES):
+                for half in range(CHUNKS // 2):
+                    bank = psum.tile([P, BANK], F32, name="bank")
+                    for u in range(2):
+                        for j in range(2):
+                            first_word = (2 * half + j) * ROW_WORDS + g * PASS_WORDS + u * P
+                            nc.tensor.transpose(
+                                out=bank[:, (2 * u + j) * P : (2 * u + j + 1) * P],
+                                in_=words[:, first_word : first_word + P],
+                                identity=ident[:],
+                            )
+                    n = g * (CHUNKS // 2) + half
+                    target = grouped_words[:, n * BANK : (n + 1) * BANK].rearrange(
+                        "p (r u) -> p r u", u=2
+                    )
+                    planes = bank[:].rearrange("p (u r) -> p r u", u=2)
+                    if n == PASSES * (CHUNKS // 2) - 1:
+                        nc.vector.tensor_copy(out=target, in_=planes)
+                    else:
+                        nc.scalar.copy(out=target, in_=planes)
+            return grouped
+
+        def quantise_rows(grouped, codes, scales):
+            for g in range(PASSES):
+                nc.vector.quantize_mx(
+                    out=codes[:, g * TOKENS : (g + 1) * TOKENS].bitcast(FP8X4),
+                    scales=scales[:, g * TOKENS : (g + 1) * TOKENS],
+                    in_=grouped[:, g * TOKENS * PACK : (g + 1) * TOKENS * PACK],
+                )
+
+        def new_unit_mx():
+            codes = unit_mx_pool.tile([P, PASSES * TOKENS], U32, name="unit_codes", align_bytes=64)
+            scales = unit_mx_pool.tile([P, PASSES * TOKENS], U8, name="unit_scales", align_bytes=64)
+            return codes, scales
+
+        def project(unit_mx, weight_mx):
+            codes, scales = unit_mx
+            w_codes, w_scales = weight_mx
+            feat = feat_pool.tile([P, TOKENS * PACK], BF16, name="feat", align_bytes=64)
+            for c in range(CHUNKS):
+                bank = psum.tile([P, BANK], F32, name="bank")
+                for t in range(PACK):
+                    for g in range(PASSES):
+                        w_cols = slice(g * FEATURES + t * P, g * FEATURES + (t + 1) * P)
+                        x_cols = slice(g * TOKENS + c * P, g * TOKENS + (c + 1) * P)
+                        nc.tensor.matmul_mx(
+                            out=bank[:, t * P : (t + 1) * P],
+                            lhsT=w_codes[:, w_cols].bitcast(FP8X4),
+                            lhsT_scale=w_scales[:, w_cols],
+                            rhs=codes[:, x_cols].bitcast(FP8X4),
+                            rhs_scale=scales[:, x_cols],
+                            start=(g == 0),
+                            stop=(g == PASSES - 1),
+                        )
+                nc.scalar.copy(
+                    out=feat[:, c * BANK : (c + 1) * BANK].rearrange("p (r t) -> p r t", t=PACK),
+                    in_=bank[:].rearrange("p (t r) -> p r t", t=PACK),
+                )
+            return feat
+
+        def quantise_features(feat):
+            codes = feat_mx_pool.tile([P, TOKENS], U32, name="feat_codes", align_bytes=64)
+            scales = feat_mx_pool.tile([P, TOKENS], U8, name="feat_scales", align_bytes=64)
+            nc.vector.quantize_mx(out=codes[:].bitcast(FP8X4), scales=scales[:], in_=feat[:])
+            return codes, scales
+
+        def build_caps():
+            for c in range(CHUNKS):
+                nc.vector.tensor_scalar(
+                    out=caps[:, c * TOKENS : (c + 1) * TOKENS],
+                    in0=mask_rows[:, 2 * c * TOKENS : 2 * (c + 1) * TOKENS : 2],
+                    scalar1=-2.0 * CAP,
+                    scalar2=CAP,
+                    op0=ALU.mult,
+                    op1=ALU.add,
+                )
+
+        def score_pair(pair, q_mx, k_mx):
+            q_codes, q_scales = q_mx
+            k_codes, k_scales = k_mx
+            prob = prob_pool.tile([P, PAIR * TOKENS], F32, name="prob")
+            negmax = small.tile([P, PAIR], F32, name="negmax")
+            for i in range(PAIR):
+                tile_no = (pair % (CHUNKS // PAIR)) * PAIR + i
+                bank = psum.tile([P, BANK], F32, name="bank")
+                nc.tensor.matmul_mx(
+                    out=bank[:],
+                    lhsT=q_codes[:, tile_no * P : (tile_no + 1) * P].bitcast(FP8X4),
+                    lhsT_scale=q_scales[:, tile_no * P : (tile_no + 1) * P],
+                    rhs=k_codes[:].bitcast(FP8X4),
+                    rhs_scale=k_scales[:],
+                    start=True,
+                    stop=True,
+                )
+                nc.vector.scalar_tensor_tensor(
+                    out=prob[:, i * TOKENS : (i + 1) * TOKENS],
+                    in0=bank[:],
+                    scalar=SCORE_SCALE,
+                    in1=caps[:, tile_no * TOKENS : (tile_no + 1) * TOKENS],
+                    op0=ALU.mult,
+                    op1=ALU.min,
+                )
+            for i in range(PAIR):
+                nc.vector.tensor_reduce(
+                    out=negmax[:, i : i + 1],
+                    in_=prob[:, i * TOKENS : (i + 1) * TOKENS],
+                    axis=mybir.AxisListType.X,
+                    op=ALU.max,
+                    negate=True,
+                )
+            return prob, negmax
+
+        def exponentials(prob, negmax):
+            rowsum = small.tile([P, PAIR], F32, name="rowsum")
+            for i in range(PAIR):
+                nc.scalar.activation(
+                    out=prob[:, i * TOKENS : (i + 1) * TOKENS],
+                    in_=prob[:, i * TOKENS : (i + 1) * TOKENS],
+                    func=ACT.Exp,
+                    bias=negmax[:, i : i + 1],
+                    scale=1.0,
+                    accum_out=rowsum[:, i : i + 1],
+                )
+            return rowsum
+
+        def normalise_and_store(pair, prob, rowsum):
+            inverse = small.tile([P, PAIR], F32, name="inverse")
+            nc.vector.reciprocal(out=inverse[:], in_=rowsum[:])
+            for i in range(PAIR):
+                tile_no = (pair % (CHUNKS // PAIR)) * PAIR + i
+                nc.vector.tensor_scalar_mul(
+                    out=prob[:, i * TOKENS : (i + 1) * TOKENS],
+                    in0=prob[:, i * TOKENS : (i + 1) * TOKENS],
+                    scalar1=inverse[:, i : i + 1],
+                )
+                nc.sync.dma_start(
+                    out=out[pair // (CHUNKS // PAIR), tile_no * P : (tile_no + 1) * P, :],
+                    in_=prob[:, i * TOKENS : (i + 1) * TOKENS],
+                )
+
+        ident = const.tile([P, P], F32, name="ident")
+        make_identity(nc, ident[:])
+        warm = const.tile([P, 1], F32, name="warm")
+        nc.vector.memset(warm[:], 0.0)
+        nc.scalar.activation(out=warm[:], in_=warm[:], func=ACT.Exp)
+
+        rows = {}
+        rotation_rows = load_weight(rotation_params)
+        rows[0] = load_unit(0)
+        entangle_rows = load_weight(entangle_params)
+        for unit in range(1, PREFETCH):
+            rows[unit] = load_unit(unit)
+        mask_rows = const.tile([P, CHUNKS * 2 * TOKENS], I32, name="mask_rows")
+        mask_words = mask.bitcast(I32)
+        for c in range(CHUNKS):
+            nc.sync.dma_start(
+                out=mask_rows[:, 2 * c * TOKENS : 2 * (c + 1) * TOKENS],
+                in_=mask_words[c * P : (c + 1) * P, :],
+            )
+        caps = const.tile([P, CHUNKS * TOKENS], F32, name="caps")
+
+        weight_mx = []
+        unit_mx = {}
+        for name in ("rotation", "entangle"):
+            weight_mx.append(
+                (
+                    const.tile([P, PASSES * FEATURES], U32, name=name + "_codes", align_bytes=64),
+                    const.tile([P, PASSES * FEATURES], U8, name=name + "_scales", align_bytes=64),
+                )
+            )
+        quantise_rows(transpose_rows(rotation_rows), weight_mx[0][0], weight_mx[0][1])
+        unit_mx[0] = new_unit_mx()
+        quantise_rows(transpose_rows(rows[0]), unit_mx[0][0], unit_mx[0][1])
+        quantise_rows(transpose_rows(entangle_rows), weight_mx[1][0], weight_mx[1][1])
+
+        feat_mx = {}
+        scored = {}
+        summed = {}
+        for step in range(UNITS + 3):
+            ahead = step + PREFETCH
+            following = step + 1
+            scoring = step - 2
+            finishing = step - 3
+            if ahead < UNITS:
+                rows[ahead] = load_unit(ahead)
+            if following < UNITS:
+                grouped = transpose_rows(rows[following])
+            if 0 <= finishing < PAIRS:
+                summed[finishing] = exponentials(scored[finishing][0], scored[finishing][1])
+            if following < UNITS:
+                unit_mx[following] = new_unit_mx()
+                quantise_rows(grouped, unit_mx[following][0], unit_mx[following][1])
+            if 0 <= finishing < PAIRS:
+                normalise_and_store(finishing, scored[finishing][0], summed[finishing])
+            if step < UNITS:
+                feat = project(unit_mx[step], weight_mx[step % 2])
+            if scoring == 0:
+                build_caps()
+            if 0 <= scoring < PAIRS:
+                b = scoring // (CHUNKS // PAIR)
+                scored[scoring] = score_pair(scoring, feat_mx[2 * b], feat_mx[2 * b + 1])
+            if step < UNITS:
+                feat_mx[step] = quantise_features(feat)

@@ -203,10 +203,13 @@ def tile_selfattention_pa_t_kernel(
             nc.vector.reciprocal(out=inverse[:], in_=rowsum[:])
             for i in range(PAIR):
                 tile_no = (pair % (CHUNKS // PAIR)) * PAIR + i
-                nc.vector.tensor_scalar_mul(
+                nc.gpsimd.tensor_scalar(
                     out=prob[:, i * TOKENS : (i + 1) * TOKENS],
                     in0=prob[:, i * TOKENS : (i + 1) * TOKENS],
                     scalar1=inverse[:, i : i + 1],
+                    scalar2=0.0,
+                    op0=ALU.mult,
+                    op1=ALU.add,
                 )
                 nc.sync.dma_start(
                     out=out[pair // (CHUNKS // PAIR), tile_no * P : (tile_no + 1) * P, :],
@@ -259,16 +262,14 @@ def tile_selfattention_pa_t_kernel(
             if ahead < UNITS:
                 rows[ahead] = load_unit(ahead)
             if following < UNITS:
-                grouped = transpose_rows(rows[following])
-            if 0 <= finishing < PAIRS:
-                summed[finishing] = exponentials(scored[finishing][0], scored[finishing][1])
-            if following < UNITS:
                 unit_mx[following] = new_unit_mx()
-                quantise_rows(grouped, unit_mx[following][0], unit_mx[following][1])
-            if 0 <= finishing < PAIRS:
-                normalise_and_store(finishing, scored[finishing][0], summed[finishing])
+                quantise_rows(
+                    transpose_rows(rows[following]), unit_mx[following][0], unit_mx[following][1]
+                )
             if step < UNITS:
                 feat = project(unit_mx[step], weight_mx[step % 2])
+            if 0 <= finishing < PAIRS:
+                summed[finishing] = exponentials(scored[finishing][0], scored[finishing][1])
             if scoring == 0:
                 build_caps()
             if 0 <= scoring < PAIRS:
@@ -276,3 +277,5 @@ def tile_selfattention_pa_t_kernel(
                 scored[scoring] = score_pair(scoring, feat_mx[2 * b], feat_mx[2 * b + 1])
             if step < UNITS:
                 feat_mx[step] = quantise_features(feat)
+            if 0 <= finishing < PAIRS:
+                normalise_and_store(finishing, scored[finishing][0], summed[finishing])

@@ -30,6 +30,8 @@ UNITS = 2 * BATCH
 PAIR = 2
 PAIRS = BATCH * CHUNKS // PAIR
 PREFETCH = 4
+UNIT_BANKS = PASSES * CHUNKS // 2
+VECTOR_EVERY = 3
 
 SCORE_SCALE = 1.0 / 32.0
 CAP = 1.0e38
@@ -67,7 +69,7 @@ def tile_selfattention_pa_t_kernel(
             by_chunk = weight.rearrange("(p c) d -> c p d", c=CHUNKS)
             return load_rows([by_chunk[c] for c in range(CHUNKS)])
 
-        def transpose_rows(rows):
+        def transpose_rows(rows, call_no):
             words = rows[:].bitcast(F32)
             grouped = grouped_pool.tile(
                 [P, PASSES * TOKENS * PACK], BF16, name="grouped", align_bytes=64
@@ -89,7 +91,7 @@ def tile_selfattention_pa_t_kernel(
                         "p (r u) -> p r u", u=2
                     )
                     planes = bank[:].rearrange("p (u r) -> p r u", u=2)
-                    if n == PASSES * (CHUNKS // 2) - 1:
+                    if (call_no * UNIT_BANKS + n) % VECTOR_EVERY == VECTOR_EVERY - 1:
                         nc.vector.tensor_copy(out=target, in_=planes)
                     else:
                         nc.scalar.copy(out=target, in_=planes)
@@ -246,10 +248,10 @@ def tile_selfattention_pa_t_kernel(
                     const.tile([P, PASSES * FEATURES], U8, name=name + "_scales", align_bytes=64),
                 )
             )
-        quantise_rows(transpose_rows(rotation_rows), weight_mx[0][0], weight_mx[0][1])
+        quantise_rows(transpose_rows(rotation_rows, 0), weight_mx[0][0], weight_mx[0][1])
         unit_mx[0] = new_unit_mx()
-        quantise_rows(transpose_rows(rows[0]), unit_mx[0][0], unit_mx[0][1])
-        quantise_rows(transpose_rows(entangle_rows), weight_mx[1][0], weight_mx[1][1])
+        quantise_rows(transpose_rows(rows[0], 1), unit_mx[0][0], unit_mx[0][1])
+        quantise_rows(transpose_rows(entangle_rows, 2), weight_mx[1][0], weight_mx[1][1])
 
         feat_mx = {}
         scored = {}
@@ -264,7 +266,9 @@ def tile_selfattention_pa_t_kernel(
             if following < UNITS:
                 unit_mx[following] = new_unit_mx()
                 quantise_rows(
-                    transpose_rows(rows[following]), unit_mx[following][0], unit_mx[following][1]
+                    transpose_rows(rows[following], following + 2),
+                    unit_mx[following][0],
+                    unit_mx[following][1],
                 )
             if step < UNITS:
                 feat = project(unit_mx[step], weight_mx[step % 2])

@@ -50,8 +50,8 @@ def tile_selfattention_pa_t_kernel(
         unit_mx_pool = ctx.enter_context(tc.tile_pool(name="unit_mx", bufs=3))
         feat_pool = ctx.enter_context(tc.tile_pool(name="feat", bufs=2))
         feat_mx_pool = ctx.enter_context(tc.tile_pool(name="feat_mx", bufs=6))
-        prob_pool = ctx.enter_context(tc.tile_pool(name="prob", bufs=4))
-        small = ctx.enter_context(tc.tile_pool(name="small", bufs=4))
+        prob_pool = ctx.enter_context(tc.tile_pool(name="prob", bufs=5))
+        small = ctx.enter_context(tc.tile_pool(name="small", bufs=5))
         psum = ctx.enter_context(tc.psum_pool(name="psum", bufs=PSUM_BANKS))
         ctx.enter_context(tc.manual_schedule())
 
@@ -98,12 +98,7 @@ def tile_selfattention_pa_t_kernel(
             return grouped
 
         def quantise_rows(grouped, codes, scales):
-            for g in range(PASSES):
-                nc.vector.quantize_mx(
-                    out=codes[:, g * TOKENS : (g + 1) * TOKENS].bitcast(FP8X4),
-                    scales=scales[:, g * TOKENS : (g + 1) * TOKENS],
-                    in_=grouped[:, g * TOKENS * PACK : (g + 1) * TOKENS * PACK],
-                )
+            nc.vector.quantize_mx(out=codes[:].bitcast(FP8X4), scales=scales[:], in_=grouped[:])
 
         def new_unit_mx():
             codes = unit_mx_pool.tile([P, PASSES * TOKENS], U32, name="unit_codes", align_bytes=64)
@@ -256,30 +251,31 @@ def tile_selfattention_pa_t_kernel(
         feat_mx = {}
         scored = {}
         summed = {}
-        for step in range(UNITS + 3):
+        feat = {}
+        for step in range(UNITS + 4):
             ahead = step + PREFETCH
             following = step + 1
+            projected = step - 1
             scoring = step - 2
-            finishing = step - 3
+            raising = step - 3
+            dividing = step - 4
             if ahead < UNITS:
                 rows[ahead] = load_unit(ahead)
             if following < UNITS:
+                grouped = transpose_rows(rows[following], following + 2)
+            if 0 <= projected < UNITS:
+                feat_mx[projected] = quantise_features(feat[projected])
+            if following < UNITS:
                 unit_mx[following] = new_unit_mx()
-                quantise_rows(
-                    transpose_rows(rows[following], following + 2),
-                    unit_mx[following][0],
-                    unit_mx[following][1],
-                )
+                quantise_rows(grouped, unit_mx[following][0], unit_mx[following][1])
+            if 0 <= dividing < PAIRS:
+                normalise_and_store(dividing, scored[dividing][0], summed[dividing])
             if step < UNITS:
-                feat = project(unit_mx[step], weight_mx[step % 2])
-            if 0 <= finishing < PAIRS:
-                summed[finishing] = exponentials(scored[finishing][0], scored[finishing][1])
+                feat[step] = project(unit_mx[step], weight_mx[step % 2])
+            if 0 <= raising < PAIRS:
+                summed[raising] = exponentials(scored[raising][0], scored[raising][1])
             if scoring == 0:
                 build_caps()
             if 0 <= scoring < PAIRS:
                 b = scoring // (CHUNKS // PAIR)
                 scored[scoring] = score_pair(scoring, feat_mx[2 * b], feat_mx[2 * b + 1])
-            if step < UNITS:
-                feat_mx[step] = quantise_features(feat)
-            if 0 <= finishing < PAIRS:
-                normalise_and_store(finishing, scored[finishing][0], summed[finishing])

from contextlib import ExitStack

import concourse.mybir as mybir
from concourse.masks import make_identity

F32 = mybir.dt.float32
BF16 = mybir.dt.bfloat16
I32 = mybir.dt.int32
U32 = mybir.dt.uint32
U8 = mybir.dt.uint8
FP8X4 = mybir.dt.float8_e4m3fn_x4
ALU = mybir.AluOpType
ACT = mybir.ActivationFunctionType

P = 128
PACK = 4
K_PASS = P * PACK
BANK = 512
PSUM_BANKS = 8

BATCH = 8
TOKENS = 512
WIDTH = 1024
FEATURES = 512
CHUNKS = TOKENS // P
PASSES = WIDTH // K_PASS
ROW_WORDS = WIDTH // 2
PASS_WORDS = K_PASS // 2
UNITS = 2 * BATCH
PAIR = 2
PAIRS = BATCH * CHUNKS // PAIR
PREFETCH = 4
UNIT_BANKS = PASSES * CHUNKS // 2
VECTOR_EVERY = 3

SCORE_SCALE = 1.0 / 32.0
CAP = 1.0e38

FLOPS = 2 * (2 * BATCH * TOKENS * WIDTH * FEATURES) + 2 * BATCH * TOKENS * TOKENS * FEATURES


def tile_selfattention_pa_t_kernel(
    tc, q_lin, k_lin, rotation_params, entangle_params, mask, out
):
    nc = tc.nc
    with ExitStack() as ctx:
        const = ctx.enter_context(tc.tile_pool(name="const", bufs=1))
        rows_pool = ctx.enter_context(tc.tile_pool(name="rows", bufs=PREFETCH + 2))
        grouped_pool = ctx.enter_context(tc.tile_pool(name="grouped", bufs=2))
        unit_mx_pool = ctx.enter_context(tc.tile_pool(name="unit_mx", bufs=3))
        feat_pool = ctx.enter_context(tc.tile_pool(name="feat", bufs=2))
        feat_mx_pool = ctx.enter_context(tc.tile_pool(name="feat_mx", bufs=6))
        prob_pool = ctx.enter_context(tc.tile_pool(name="prob", bufs=5))
        small = ctx.enter_context(tc.tile_pool(name="small", bufs=5))
        psum = ctx.enter_context(tc.psum_pool(name="psum", bufs=PSUM_BANKS))
        ctx.enter_context(tc.manual_schedule())

        def load_rows(chunk_views):
            rows = rows_pool.tile([P, CHUNKS * WIDTH], BF16, name="rows")
            for c in range(CHUNKS):
                nc.sync.dma_start(out=rows[:, c * WIDTH : (c + 1) * WIDTH], in_=chunk_views[c])
            return rows

        def load_unit(unit):
            source = q_lin if unit % 2 == 0 else k_lin
            return load_rows([source[unit // 2, c * P : (c + 1) * P, :] for c in range(CHUNKS)])

        def load_weight(weight):
            by_chunk = weight.rearrange("(p c) d -> c p d", c=CHUNKS)
            return load_rows([by_chunk[c] for c in range(CHUNKS)])

        def transpose_rows(rows, call_no):
            words = rows[:].bitcast(F32)
            grouped = grouped_pool.tile(
                [P, PASSES * TOKENS * PACK], BF16, name="grouped", align_bytes=64
            )
            grouped_words = grouped[:].bitcast(F32)
            for g in range(PASSES):
                for half in range(CHUNKS // 2):
                    bank = psum.tile([P, BANK], F32, name="bank")
                    for u in range(2):
                        for j in range(2):
                            first_word = (2 * half + j) * ROW_WORDS + g * PASS_WORDS + u * P
                            nc.tensor.transpose(
                                out=bank[:, (2 * u + j) * P : (2 * u + j + 1) * P],
                                in_=words[:, first_word : first_word + P],
                                identity=ident[:],
                            )
                    n = g * (CHUNKS // 2) + half
                    target = grouped_words[:, n * BANK : (n + 1) * BANK].rearrange(
                        "p (r u) -> p r u", u=2
                    )
                    planes = bank[:].rearrange("p (u r) -> p r u", u=2)
                    if (call_no * UNIT_BANKS + n) % VECTOR_EVERY == VECTOR_EVERY - 1:
                        nc.vector.tensor_copy(out=target, in_=planes)
                    else:
                        nc.scalar.copy(out=target, in_=planes)
            return grouped

        def quantise_rows(grouped, codes, scales):
            nc.vector.quantize_mx(out=codes[:].bitcast(FP8X4), scales=scales[:], in_=grouped[:])

        def new_unit_mx():
            codes = unit_mx_pool.tile([P, PASSES * TOKENS], U32, name="unit_codes", align_bytes=64)
            scales = unit_mx_pool.tile([P, PASSES * TOKENS], U8, name="unit_scales", align_bytes=64)
            return codes, scales

        def project(unit_mx, weight_mx):
            codes, scales = unit_mx
            w_codes, w_scales = weight_mx
            feat = feat_pool.tile([P, TOKENS * PACK], BF16, name="feat", align_bytes=64)
            for c in range(CHUNKS):
                bank = psum.tile([P, BANK], F32, name="bank")
                for t in range(PACK):
                    for g in range(PASSES):
                        w_cols = slice(g * FEATURES + t * P, g * FEATURES + (t + 1) * P)
                        x_cols = slice(g * TOKENS + c * P, g * TOKENS + (c + 1) * P)
                        nc.tensor.matmul_mx(
                            out=bank[:, t * P : (t + 1) * P],
                            lhsT=w_codes[:, w_cols].bitcast(FP8X4),
                            lhsT_scale=w_scales[:, w_cols],
                            rhs=codes[:, x_cols].bitcast(FP8X4),
                            rhs_scale=scales[:, x_cols],
                            start=(g == 0),
                            stop=(g == PASSES - 1),
                        )
                nc.scalar.copy(
                    out=feat[:, c * BANK : (c + 1) * BANK].rearrange("p (r t) -> p r t", t=PACK),
                    in_=bank[:].rearrange("p (t r) -> p r t", t=PACK),
                )
            return feat

        def quantise_features(feat):
            codes = feat_mx_pool.tile([P, TOKENS], U32, name="feat_codes", align_bytes=64)
            scales = feat_mx_pool.tile([P, TOKENS], U8, name="feat_scales", align_bytes=64)
            nc.vector.quantize_mx(out=codes[:].bitcast(FP8X4), scales=scales[:], in_=feat[:])
            return codes, scales

        def build_caps():
            for c in range(CHUNKS):
                nc.vector.tensor_scalar(
                    out=caps[:, c * TOKENS : (c + 1) * TOKENS],
                    in0=mask_rows[:, 2 * c * TOKENS : 2 * (c + 1) * TOKENS : 2],
                    scalar1=-2.0 * CAP,
                    scalar2=CAP,
                    op0=ALU.mult,
                    op1=ALU.add,
                )

        def score_pair(pair, q_mx, k_mx):
            q_codes, q_scales = q_mx
            k_codes, k_scales = k_mx
            prob = prob_pool.tile([P, PAIR * TOKENS], F32, name="prob")
            negmax = small.tile([P, PAIR], F32, name="negmax")
            for i in range(PAIR):
                tile_no = (pair % (CHUNKS // PAIR)) * PAIR + i
                bank = psum.tile([P, BANK], F32, name="bank")
                nc.tensor.matmul_mx(
                    out=bank[:],
                    lhsT=q_codes[:, tile_no * P : (tile_no + 1) * P].bitcast(FP8X4),
                    lhsT_scale=q_scales[:, tile_no * P : (tile_no + 1) * P],
                    rhs=k_codes[:].bitcast(FP8X4),
                    rhs_scale=k_scales[:],
                    start=True,
                    stop=True,
                )
                nc.vector.scalar_tensor_tensor(
                    out=prob[:, i * TOKENS : (i + 1) * TOKENS],
                    in0=bank[:],
                    scalar=SCORE_SCALE,
                    in1=caps[:, tile_no * TOKENS : (tile_no + 1) * TOKENS],
                    op0=ALU.mult,
                    op1=ALU.min,
                )
            for i in range(PAIR):
                nc.vector.tensor_reduce(
                    out=negmax[:, i : i + 1],
                    in_=prob[:, i * TOKENS : (i + 1) * TOKENS],
                    axis=mybir.AxisListType.X,
                    op=ALU.max,
                    negate=True,
                )
            return prob, negmax

        def exponentials(prob, negmax):
            rowsum = small.tile([P, PAIR], F32, name="rowsum")
            for i in range(PAIR):
                nc.scalar.activation(
                    out=prob[:, i * TOKENS : (i + 1) * TOKENS],
                    in_=prob[:, i * TOKENS : (i + 1) * TOKENS],
                    func=ACT.Exp,
                    bias=negmax[:, i : i + 1],
                    scale=1.0,
                    accum_out=rowsum[:, i : i + 1],
                )
            return rowsum

        def normalise_and_store(pair, prob, rowsum):
            inverse = small.tile([P, PAIR], F32, name="inverse")
            nc.vector.reciprocal(out=inverse[:], in_=rowsum[:])
            for i in range(PAIR):
                tile_no = (pair % (CHUNKS // PAIR)) * PAIR + i
                nc.gpsimd.tensor_scalar(
                    out=prob[:, i * TOKENS : (i + 1) * TOKENS],
                    in0=prob[:, i * TOKENS : (i + 1) * TOKENS],
                    scalar1=inverse[:, i : i + 1],
                    scalar2=0.0,
                    op0=ALU.mult,
                    op1=ALU.add,
                )
                nc.sync.dma_start(
                    out=out[pair // (CHUNKS // PAIR), tile_no * P : (tile_no + 1) * P, :],
                    in_=prob[:, i * TOKENS : (i + 1) * TOKENS],
                )

        ident = const.tile([P, P], F32, name="ident")
        make_identity(nc, ident[:])
        warm = const.tile([P, 1], F32, name="warm")
        nc.vector.memset(warm[:], 0.0)
        nc.scalar.activation(out=warm[:], in_=warm[:], func=ACT.Exp)

        rows = {}
        rotation_rows = load_weight(rotation_params)
        rows[0] = load_unit(0)
        entangle_rows = load_weight(entangle_params)
        for unit in range(1, PREFETCH):
            rows[unit] = load_unit(unit)
        mask_rows = const.tile([P, CHUNKS * 2 * TOKENS], I32, name="mask_rows")
        mask_words = mask.bitcast(I32)
        for c in range(CHUNKS):
            nc.sync.dma_start(
                out=mask_rows[:, 2 * c * TOKENS : 2 * (c + 1) * TOKENS],
                in_=mask_words[c * P : (c + 1) * P, :],
            )
        caps = const.tile([P, CHUNKS * TOKENS], F32, name="caps")

        weight_mx = []
        unit_mx = {}
        for name in ("rotation", "entangle"):
            weight_mx.append(
                (
                    const.tile([P, PASSES * FEATURES], U32, name=name + "_codes", align_bytes=64),
                    const.tile([P, PASSES * FEATURES], U8, name=name + "_scales", align_bytes=64),
                )
            )
        quantise_rows(transpose_rows(rotation_rows, 0), weight_mx[0][0], weight_mx[0][1])
        unit_mx[0] = new_unit_mx()
        quantise_rows(transpose_rows(rows[0], 1), unit_mx[0][0], unit_mx[0][1])
        quantise_rows(transpose_rows(entangle_rows, 2), weight_mx[1][0], weight_mx[1][1])

        feat_mx = {}
        scored = {}
        summed = {}
        feat = {}
        for step in range(UNITS + 4):
            ahead = step + PREFETCH
            following = step + 1
            projected = step - 1
            scoring = step - 2
            raising = step - 3
            dividing = step - 4
            if ahead < UNITS:
                rows[ahead] = load_unit(ahead)
            if following < UNITS:
                grouped = transpose_rows(rows[following], following + 2)
            if 0 <= projected < UNITS:
                feat_mx[projected] = quantise_features(feat[projected])
            if following < UNITS:
                unit_mx[following] = new_unit_mx()
                quantise_rows(grouped, unit_mx[following][0], unit_mx[following][1])
            if 0 <= dividing < PAIRS:
                normalise_and_store(dividing, scored[dividing][0], summed[dividing])
            if step < UNITS:
                feat[step] = project(unit_mx[step], weight_mx[step % 2])
            if 0 <= raising < PAIRS:
                summed[raising] = exponentials(scored[raising][0], scored[raising][1])
            if scoring == 0:
                build_caps()
            if 0 <= scoring < PAIRS:
                b = scoring // (CHUNKS // PAIR)
                scored[scoring] = score_pair(scoring, feat_mx[2 * b], feat_mx[2 * b + 1])
